import numpy as np
import ml_dtypes

BF16 = ml_dtypes.bfloat16


def bf(x):
    return np.asarray(x, np.float32).astype(BF16)


def f32(x):
    return np.asarray(x, np.float32)


def f64(x):
    return np.asarray(x).astype(np.float64)


def striped(idx):
    return np.tile(idx.reshape(-1, 16).T, (8, 1))


S, D, R, H0, M, E, N = 4096, 128, 128, 4096, 512, 1024, 2048
CUTOFF = 5.0
NORM = np.sqrt(2.0 / CUTOFF)
RS = NORM * R / CUTOFF


def silu(v):
    return v / (1.0 + np.exp(-v))


def setup_inputs():
    table = bf(np.random.standard_normal((S, D)))
    w_lin = bf(np.concatenate([np.random.standard_normal((2 * D, M)) / np.sqrt(3 * D), np.random.standard_normal((H0, M)) / np.sqrt(H0)], axis=0))
    b_lin = f32(0.2 * np.random.standard_normal((M, 1)))
    d = f32((CUTOFF / R) * (0.1 + 0.85 * np.random.random_sample((1, E))))
    freq = f32(np.arange(1, R + 1)[:, None] * (np.pi / CUTOFF))
    w_rbf0 = bf(np.random.standard_normal((R, H0)) / (RS * np.sqrt(R)))
    b_rbf0 = f32(0.2 * np.random.standard_normal((H0, 1)))
    w_rbf1 = bf(np.random.standard_normal((R, M)) / (RS * np.sqrt(R)))
    idx = np.random.permutation(np.tile(np.arange(S), 2))[:N]
    return {"table": table, "w_lin": w_lin, "b_lin": b_lin, "d": d, "freq": freq, "w_rbf0": w_rbf0, "b_rbf0": b_rbf0, "w_rbf1": w_rbf1, "offs": striped(idx)}


def reference(table, w_lin, b_lin, d, freq, w_rbf0, b_rbf0, w_rbf1, offs):
    idx = offs[:16].T.reshape(-1)
    src, dst = idx[:E], idx[E:]
    rbf = NORM * np.sin(f64(freq) * f64(d)) / f64(d)
    rbf0 = silu(f64(w_rbf0).T @ rbf + f64(b_rbf0))
    t = f64(table)
    wl = f64(w_lin)
    h = wl[:D].T @ t[src].T + wl[D:2 * D].T @ t[dst].T + wl[2 * D:].T @ rbf0 + f64(b_lin)
    e1 = silu(h)
    return (f64(w_rbf1).T @ rbf) * e1

@@ -1,0 +1,156 @@
+import concourse.mybir as mybir
+from concourse.masks import make_identity
+
+BF16 = mybir.dt.bfloat16
+F32 = mybir.dt.float32
+U16 = mybir.dt.uint16
+FUNC = mybir.ActivationFunctionType
+MULT = mybir.AluOpType.mult
+
+P = 128
+NODES = 4096
+FEAT = 128
+RADIAL = 128
+HIDDEN = 4096
+OUT_FEAT = 512
+EDGES = 1024
+NORM = (2.0 / 5.0) ** 0.5
+
+PIECE = 512
+N_PIECES = EDGES // PIECE
+PIECE_COLS = PIECE // 16
+HID_BLOCKS = HIDDEN // P
+OUT_BLOCKS = OUT_FEAT // P
+ROWS_EACH = 8
+STAGE_ROWS = P * ROWS_EACH
+N_STAGES = NODES // STAGE_ROWS
+W_CHUNK = 4
+AHEAD = 2
+
+FLOPS = 2 * EDGES * (RADIAL * HIDDEN + (2 * FEAT + HIDDEN) * OUT_FEAT + RADIAL * OUT_FEAT)
+
+
+def tile_edgefeatureinit_b_kernel(tc, table, w_lin, b_lin, d, freq, w_rbf0, b_rbf0, w_rbf1, offs, out):
+    nc = tc.nc
+    with (
+        tc.tile_pool(name="held", bufs=1) as held,
+        tc.tile_pool(name="hidden_ring", bufs=4) as hidden_ring,
+        tc.tile_pool(name="result_ring", bufs=2) as result_ring,
+        tc.psum_pool(name="hidden_psum", bufs=3) as hidden_psum,
+        tc.psum_pool(name="second_psum", bufs=1) as second_psum,
+    ):
+        offsets = held.tile([P, 2 * EDGES // 16], U16, name="offsets")
+        nc.sync.dma_start(offsets[:], offs)
+
+        d_all = held.tile([P, EDGES], F32, name="d_all")
+        nc.sync.dma_start(d_all[:], d.rearrange("o e -> (o e)").partition_broadcast(P))
+        freq_sb = held.tile([P, 1], F32, name="freq_sb")
+        nc.scalar.dma_start(freq_sb[:], freq)
+
+        identity = held.tile([P, P], BF16, name="identity")
+        make_identity(nc, identity[:])
+
+        stages = []
+        for g in range(N_STAGES):
+            stage = held.tile([P, ROWS_EACH * FEAT], BF16, name="stage%d" % g)
+            rows = table[g * STAGE_ROWS:(g + 1) * STAGE_ROWS, :]
+            nc.sync.dma_start(stage[:], rows.rearrange("(p b) k -> p (b k)", b=ROWS_EACH))
+            stages.append(stage)
+
+        w_rbf0_sb = held.tile([P, HIDDEN], BF16, name="w_rbf0_sb")
+        nc.gpsimd.dma_start(w_rbf0_sb[:], w_rbf0)
+        w_rbf0_blocks = w_rbf0_sb[:].rearrange("r (p a) -> r a p", a=HID_BLOCKS)
+        b_rbf0_sb = held.tile([P, HID_BLOCKS], F32, name="b_rbf0_sb")
+        nc.scalar.dma_start(b_rbf0_sb[:], b_rbf0.rearrange("(p a) o -> p (a o)", a=HID_BLOCKS))
+        w_rbf1_sb = held.tile([P, OUT_FEAT], BF16, name="w_rbf1_sb")
+        nc.scalar.dma_start(w_rbf1_sb[:], w_rbf1)
+
+        w_hidden_rows = w_lin[2 * FEAT:, :].rearrange("(p a) m -> p a m", a=HID_BLOCKS)
+        w_hidden = []
+        for g in range(HID_BLOCKS // W_CHUNK):
+            chunk = held.tile([P, W_CHUNK, OUT_FEAT], BF16, name="w_hidden%d" % g)
+            nc.sync.dma_start(chunk[:], w_hidden_rows[:, g * W_CHUNK:(g + 1) * W_CHUNK, :])
+            w_hidden.append(chunk)
+
+        w_node = held.tile([P, 2, OUT_FEAT], BF16, name="w_node")
+        nc.gpsimd.dma_start(w_node[:], w_lin[0:2 * FEAT, :].rearrange("(s k) m -> k s m", s=2))
+        b_lin_sb = held.tile([P, OUT_BLOCKS], F32, name="b_lin_sb")
+        with nc.allow_non_contiguous_dma(reason="512 bias values, one to a partition and block"):
+            nc.scalar.dma_start(b_lin_sb[:], b_lin.rearrange("(a p) o -> p (a o)", p=P))
+
+        sine = held.tile([P, EDGES], F32, name="sine")
+        nc.scalar.activation(sine[:], d_all[:], FUNC.Sin, scale=freq_sb[:, 0:1])
+        inv_d = held.tile([P, EDGES], F32, name="inv_d")
+        rbf = [held.tile([P, PIECE], BF16, name="rbf%d" % c) for c in range(N_PIECES)]
+
+        def radial_basis(c):
+            cols = slice(c * PIECE, (c + 1) * PIECE)
+            nc.vector.reciprocal(inv_d[:, cols], d_all[:, cols])
+            nc.vector.scalar_tensor_tensor(
+                out=rbf[c][:], in0=sine[:, cols], scalar=NORM, in1=inv_d[:, cols], op0=MULT, op1=MULT
+            )
+
+        radial_basis(0)
+
+        table_T = held.tile([P, NODES], BF16, name="table_T")
+        with tc.psum_pool(name="flip_psum", bufs=N_STAGES) as flip_psum:
+            for g in range(N_STAGES):
+                flipped = flip_psum.tile([P, ROWS_EACH, P], BF16, name="flipped")
+                for b in range(ROWS_EACH):
+                    nc.tensor.transpose(flipped[:, b, :], stages[g][:, b * FEAT:(b + 1) * FEAT], identity[:])
+                in_order = table_T[:, g * STAGE_ROWS:(g + 1) * STAGE_ROWS].rearrange("k (p b) -> k p b", b=ROWS_EACH)
+                if g < N_STAGES // 2:
+                    nc.scalar.copy(in_order, flipped[:].rearrange("k b p -> k p b"))
+                else:
+                    nc.vector.tensor_copy(in_order, flipped[:].rearrange("k b p -> k p b"))
+
+        radial_basis(1)
+
+        def hidden_block(c, a):
+            pre = hidden_psum.tile([P, PIECE], F32, name="pre")
+            nc.tensor.matmul(pre[:], w_rbf0_blocks[:, a, :], rbf[c][:], start=True, stop=True)
+            rbf0 = hidden_ring.tile([P, PIECE], BF16, name="rbf0")
+            nc.scalar.activation(rbf0[:], pre[:], FUNC.Silu, bias=b_rbf0_sb[:, a:a + 1])
+            return rbf0
+
+        steps = [(c, a) for c in range(N_PIECES) for a in range(HID_BLOCKS)]
+        waiting = [hidden_block(c, a) for (c, a) in steps[:AHEAD]]
+
+        with tc.psum_pool(name="acc_psum", bufs=1) as acc_psum:
+            for t, (c, a) in enumerate(steps):
+                if t + AHEAD < len(steps):
+                    waiting.append(hidden_block(*steps[t + AHEAD]))
+
+                if a == 0:
+                    acc = [acc_psum.tile([P, PIECE], F32, name="acc%d" % m) for m in range(OUT_BLOCKS)]
+                    q_sb = held.tile([P, OUT_BLOCKS, PIECE], F32, name="q_sb%d" % c)
+
+                if a < OUT_BLOCKS:
+                    q_ps = second_psum.tile([P, PIECE], F32, name="q_ps")
+                    nc.tensor.matmul(q_ps[:], w_rbf1_sb[:, a * P:(a + 1) * P], rbf[c][:], start=True, stop=True)
+                    nc.vector.tensor_copy(q_sb[:, a, :], q_ps[:])
+
+                rbf0 = waiting[t]
+                for m in range(OUT_BLOCKS):
+                    nc.tensor.matmul(
+                        acc[m][:], w_hidden[a // W_CHUNK][:, a % W_CHUNK, m * P:(m + 1) * P], rbf0[:],
+                        start=(a == 0), stop=False,
+                    )
+
+                if a == HID_BLOCKS - 1:
+                    source = offsets[:, c * PIECE_COLS:(c + 1) * PIECE_COLS]
+                    target = offsets[:, (N_PIECES + c) * PIECE_COLS:(N_PIECES + c + 1) * PIECE_COLS]
+                    for m in range(OUT_BLOCKS):
+                        nc.tensor.matmul(
+                            acc[m][:], w_node[:, 0, m * P:(m + 1) * P], table_T[:].indirect(source),
+                            start=False, stop=False,
+                        )
+                        nc.tensor.matmul(
+                            acc[m][:], w_node[:, 1, m * P:(m + 1) * P], table_T[:].indirect(target),
+                            start=False, stop=True,
+                        )
+                        e1 = result_ring.tile([P, PIECE], F32, name="e1")
+                        nc.scalar.activation(e1[:], acc[m][:], FUNC.Silu, bias=b_lin_sb[:, m:m + 1])
+                        product = result_ring.tile([P, PIECE], F32, name="product")
+                        nc.vector.tensor_tensor(product[:], e1[:], q_sb[:, m, :], MULT)
+                        nc.sync.dma_start(out[m * P:(m + 1) * P, c * PIECE:(c + 1) * PIECE], product[:])

@@ -19,12 +19,12 @@ NORM = (2.0 / 5.0) ** 0.5
 PIECE = 512
 N_PIECES = EDGES // PIECE
 PIECE_COLS = PIECE // 16
-HID_BLOCKS = HIDDEN // P
 OUT_BLOCKS = OUT_FEAT // P
-ROWS_EACH = 8
-STAGE_ROWS = P * ROWS_EACH
-N_STAGES = NODES // STAGE_ROWS
-W_CHUNK = 4
+FOUR = 4
+GROUP = FOUR * P
+N_STAGES = NODES // GROUP
+N_CHUNKS = HIDDEN // GROUP
+HID_BLOCKS = HIDDEN // P
 AHEAD = 2
 
 FLOPS = 2 * EDGES * (RADIAL * HIDDEN + (2 * FEAT + HIDDEN) * OUT_FEAT + RADIAL * OUT_FEAT)
@@ -35,122 +35,132 @@ def tile_edgefeatureinit_b_kernel(tc, table, w_lin, b_lin, d, freq, w_rbf0, b_rb
     with (
         tc.tile_pool(name="held", bufs=1) as held,
         tc.tile_pool(name="hidden_ring", bufs=4) as hidden_ring,
-        tc.tile_pool(name="result_ring", bufs=2) as result_ring,
-        tc.psum_pool(name="hidden_psum", bufs=3) as hidden_psum,
-        tc.psum_pool(name="second_psum", bufs=1) as second_psum,
+        tc.tile_pool(name="result_ring", bufs=4) as result_ring,
+        tc.psum_pool(name="acc_psum", bufs=1) as acc_psum,
+        tc.psum_pool(name="pre_psum", bufs=2) as pre_psum,
+        tc.psum_pool(name="side_psum", bufs=2) as side_psum,
     ):
-        offsets = held.tile([P, 2 * EDGES // 16], U16, name="offsets")
-        nc.sync.dma_start(offsets[:], offs)
 
-        d_all = held.tile([P, EDGES], F32, name="d_all")
-        nc.sync.dma_start(d_all[:], d.rearrange("o e -> (o e)").partition_broadcast(P))
-        freq_sb = held.tile([P, 1], F32, name="freq_sb")
-        nc.scalar.dma_start(freq_sb[:], freq)
+        d_col = held.tile([P, N_PIECES, FOUR], F32, name="d_col")
+        nc.sync.dma_start(d_col[:], d.rearrange("o (c p i) -> p c (o i)", c=N_PIECES, i=FOUR))
+        freq_row = held.tile([P, RADIAL], F32, name="freq_row")
+        nc.scalar.dma_start(freq_row[:], freq.rearrange("r o -> (r o)").partition_broadcast(P))
+
+        scratch = held.tile([P, 2], F32, name="scratch")
+        nc.vector.memset(scratch[:], 0.0)
+
+        def load_table_of(func):
+            nc.scalar.activation(scratch[:, 1:2], scratch[:, 0:1], func)
+
+        load_table_of(FUNC.Silu)
 
         identity = held.tile([P, P], BF16, name="identity")
         make_identity(nc, identity[:])
 
+        b_rbf0_sb = held.tile([P, N_CHUNKS, FOUR], F32, name="b_rbf0_sb")
+        w_rbf1_sb = held.tile([P, OUT_FEAT], BF16, name="w_rbf1_sb")
+
+        assert N_STAGES == N_CHUNKS
+        w_first = []
+        w_hidden = []
         stages = []
-        for g in range(N_STAGES):
-            stage = held.tile([P, ROWS_EACH * FEAT], BF16, name="stage%d" % g)
-            rows = table[g * STAGE_ROWS:(g + 1) * STAGE_ROWS, :]
-            nc.sync.dma_start(stage[:], rows.rearrange("(p b) k -> p (b k)", b=ROWS_EACH))
+        for g in range(N_CHUNKS):
+            first = held.tile([P, GROUP], BF16, name="w_first%d" % g)
+            nc.sync.dma_start(first[:], w_rbf0[:, g * GROUP:(g + 1) * GROUP])
+            w_first.append(first[:].rearrange("r (p a) -> r a p", a=FOUR))
+            if g == 0:
+                nc.sync.dma_start(b_rbf0_sb[:], b_rbf0.rearrange("(g p a) o -> p g (a o)", g=N_CHUNKS, a=FOUR))
+                nc.sync.dma_start(w_rbf1_sb[:], w_rbf1)
+            hidden_rows = held.tile([P, FOUR, OUT_FEAT], BF16, name="w_hidden%d" % g)
+            rows = w_lin[2 * FEAT + g * GROUP:2 * FEAT + (g + 1) * GROUP, :]
+            nc.sync.dma_start(hidden_rows[:], rows.rearrange("(p a) m -> p a m", a=FOUR))
+            w_hidden.append(hidden_rows)
+            stage = held.tile([P, FOUR, FEAT], BF16, name="stage%d" % g)
+            nc.sync.dma_start(stage[:], table[g * GROUP:(g + 1) * GROUP, :].rearrange("(p i) k -> p i k", i=FOUR))
             stages.append(stage)
 
-        w_rbf0_sb = held.tile([P, HIDDEN], BF16, name="w_rbf0_sb")
-        nc.gpsimd.dma_start(w_rbf0_sb[:], w_rbf0)
-        w_rbf0_blocks = w_rbf0_sb[:].rearrange("r (p a) -> r a p", a=HID_BLOCKS)
-        b_rbf0_sb = held.tile([P, HID_BLOCKS], F32, name="b_rbf0_sb")
-        nc.scalar.dma_start(b_rbf0_sb[:], b_rbf0.rearrange("(p a) o -> p (a o)", a=HID_BLOCKS))
-        w_rbf1_sb = held.tile([P, OUT_FEAT], BF16, name="w_rbf1_sb")
-        nc.scalar.dma_start(w_rbf1_sb[:], w_rbf1)
-
-        w_hidden_rows = w_lin[2 * FEAT:, :].rearrange("(p a) m -> p a m", a=HID_BLOCKS)
-        w_hidden = []
-        for g in range(HID_BLOCKS // W_CHUNK):
-            chunk = held.tile([P, W_CHUNK, OUT_FEAT], BF16, name="w_hidden%d" % g)
-            nc.sync.dma_start(chunk[:], w_hidden_rows[:, g * W_CHUNK:(g + 1) * W_CHUNK, :])
-            w_hidden.append(chunk)
-
+        offsets = held.tile([P, 2 * EDGES // 16], U16, name="offsets")
+        nc.sync.dma_start(offsets[:], offs)
         w_node = held.tile([P, 2, OUT_FEAT], BF16, name="w_node")
-        nc.gpsimd.dma_start(w_node[:], w_lin[0:2 * FEAT, :].rearrange("(s k) m -> k s m", s=2))
+        nc.sync.dma_start(w_node[:], w_lin[0:2 * FEAT, :].rearrange("(s k) m -> k s m", s=2))
         b_lin_sb = held.tile([P, OUT_BLOCKS], F32, name="b_lin_sb")
         with nc.allow_non_contiguous_dma(reason="512 bias values, one to a partition and block"):
-            nc.scalar.dma_start(b_lin_sb[:], b_lin.rearrange("(a p) o -> p (a o)", p=P))
+            nc.sync.dma_start(b_lin_sb[:], b_lin.rearrange("(a p) o -> p (a o)", p=P))
 
-        sine = held.tile([P, EDGES], F32, name="sine")
-        nc.scalar.activation(sine[:], d_all[:], FUNC.Sin, scale=freq_sb[:, 0:1])
-        inv_d = held.tile([P, EDGES], F32, name="inv_d")
+        def flip_four(blocks, flipped, psum, tag):
+            bank = psum.tile([P, FOUR, P], BF16, name="flip_ps", tag=tag)
+            for i in range(FOUR):
+                nc.tensor.transpose(bank[:, i, :], blocks[:, i, :], identity[:])
+            nc.vector.tensor_copy(flipped.rearrange("k (p i) -> k p i", i=FOUR), bank[:].rearrange("k i p -> k p i"))
+
+        inv_d = held.tile([P, N_PIECES, FOUR], F32, name="inv_d")
+        nc.vector.reciprocal(inv_d[:], d_col[:])
+        sine = held.tile([P, N_PIECES, FOUR, RADIAL], F32, name="sine")
+        for c in range(N_PIECES):
+            for i in range(FOUR):
+                nc.scalar.activation(sine[:, c, i, :], freq_row[:], FUNC.Sin, scale=d_col[:, c, i:i + 1])
         rbf = [held.tile([P, PIECE], BF16, name="rbf%d" % c) for c in range(N_PIECES)]
 
         def radial_basis(c):
-            cols = slice(c * PIECE, (c + 1) * PIECE)
-            nc.vector.reciprocal(inv_d[:, cols], d_all[:, cols])
-            nc.vector.scalar_tensor_tensor(
-                out=rbf[c][:], in0=sine[:, cols], scalar=NORM, in1=inv_d[:, cols], op0=MULT, op1=MULT
-            )
+            by_edge = held.tile([P, FOUR, RADIAL], BF16, name="by_edge%d" % c)
+            for i in range(FOUR):
+                nc.vector.tensor_scalar(
+                    out=by_edge[:, i, :], in0=sine[:, c, i, :], scalar1=inv_d[:, c, i:i + 1], scalar2=NORM,
+                    op0=MULT, op1=MULT,
+                )
+            flip_four(by_edge, rbf[c][:], acc_psum, "acc%d" % c)
 
-        radial_basis(0)
-
-        table_T = held.tile([P, NODES], BF16, name="table_T")
-        with tc.psum_pool(name="flip_psum", bufs=N_STAGES) as flip_psum:
-            for g in range(N_STAGES):
-                flipped = flip_psum.tile([P, ROWS_EACH, P], BF16, name="flipped")
-                for b in range(ROWS_EACH):
-                    nc.tensor.transpose(flipped[:, b, :], stages[g][:, b * FEAT:(b + 1) * FEAT], identity[:])
-                in_order = table_T[:, g * STAGE_ROWS:(g + 1) * STAGE_ROWS].rearrange("k (p b) -> k p b", b=ROWS_EACH)
-                if g < N_STAGES // 2:
-                    nc.scalar.copy(in_order, flipped[:].rearrange("k b p -> k p b"))
-                else:
-                    nc.vector.tensor_copy(in_order, flipped[:].rearrange("k b p -> k p b"))
-
-        radial_basis(1)
-
-        def hidden_block(c, a):
-            pre = hidden_psum.tile([P, PIECE], F32, name="pre")
-            nc.tensor.matmul(pre[:], w_rbf0_blocks[:, a, :], rbf[c][:], start=True, stop=True)
+        def hidden_block(c, b):
+            g, a = divmod(b, FOUR)
+            pre = pre_psum.tile([P, PIECE], F32, name="pre")
+            nc.tensor.matmul(pre[:], w_first[g][:, a, :], rbf[c][:], start=True, stop=True)
             rbf0 = hidden_ring.tile([P, PIECE], BF16, name="rbf0")
-            nc.scalar.activation(rbf0[:], pre[:], FUNC.Silu, bias=b_rbf0_sb[:, a:a + 1])
+            nc.scalar.activation(rbf0[:], pre[:], FUNC.Silu, bias=b_rbf0_sb[:, g, a:a + 1])
             return rbf0
 
-        steps = [(c, a) for c in range(N_PIECES) for a in range(HID_BLOCKS)]
-        waiting = [hidden_block(c, a) for (c, a) in steps[:AHEAD]]
+        table_T = held.tile([P, NODES], BF16, name="table_T")
+        steps = [(c, b) for c in range(N_PIECES) for b in range(HID_BLOCKS)]
+        radial_basis(0)
+        waiting = [hidden_block(c, b) for (c, b) in steps[:AHEAD]]
+        radial_basis(1)
 
-        with tc.psum_pool(name="acc_psum", bufs=1) as acc_psum:
-            for t, (c, a) in enumerate(steps):
-                if t + AHEAD < len(steps):
-                    waiting.append(hidden_block(*steps[t + AHEAD]))
+        for t, (c, b) in enumerate(steps):
+            if t + AHEAD < len(steps):
+                waiting.append(hidden_block(*steps[t + AHEAD]))
 
-                if a == 0:
-                    acc = [acc_psum.tile([P, PIECE], F32, name="acc%d" % m) for m in range(OUT_BLOCKS)]
-                    q_sb = held.tile([P, OUT_BLOCKS, PIECE], F32, name="q_sb%d" % c)
+            if b == 0:
+                acc = [acc_psum.tile([P, PIECE], F32, name="acc%d" % m) for m in range(OUT_BLOCKS)]
+                q_sb = held.tile([P, OUT_BLOCKS, PIECE], F32, name="q_sb%d" % c)
 
-                if a < OUT_BLOCKS:
-                    q_ps = second_psum.tile([P, PIECE], F32, name="q_ps")
-                    nc.tensor.matmul(q_ps[:], w_rbf1_sb[:, a * P:(a + 1) * P], rbf[c][:], start=True, stop=True)
-                    nc.vector.tensor_copy(q_sb[:, a, :], q_ps[:])
+            if c == 0 and b < N_STAGES:
+                flip_four(stages[b], table_T[:, b * GROUP:(b + 1) * GROUP], side_psum, "side")
+            if b < OUT_BLOCKS:
+                q_ps = side_psum.tile([P, PIECE], F32, name="q_ps", tag="side")
+                nc.tensor.matmul(
+                    q_ps[:], w_rbf1_sb[:, b * P:(b + 1) * P], rbf[c][:], start=True, stop=True
+                )
+                nc.vector.tensor_copy(q_sb[:, b, :], q_ps[:])
 
-                rbf0 = waiting[t]
+            for m in range(OUT_BLOCKS):
+                nc.tensor.matmul(
+                    acc[m][:], w_hidden[b // FOUR][:, b % FOUR, m * P:(m + 1) * P], waiting[t][:],
+                    start=(b == 0), stop=False,
+                )
+
+            if b == HID_BLOCKS - 1:
+                source = offsets[:, c * PIECE_COLS:(c + 1) * PIECE_COLS]
+                target = offsets[:, (N_PIECES + c) * PIECE_COLS:(N_PIECES + c + 1) * PIECE_COLS]
                 for m in range(OUT_BLOCKS):
                     nc.tensor.matmul(
-                        acc[m][:], w_hidden[a // W_CHUNK][:, a % W_CHUNK, m * P:(m + 1) * P], rbf0[:],
-                        start=(a == 0), stop=False,
+                        acc[m][:], w_node[:, 0, m * P:(m + 1) * P], table_T[:].indirect(source),
+                        start=False, stop=False,
                     )
-
-                if a == HID_BLOCKS - 1:
-                    source = offsets[:, c * PIECE_COLS:(c + 1) * PIECE_COLS]
-                    target = offsets[:, (N_PIECES + c) * PIECE_COLS:(N_PIECES + c + 1) * PIECE_COLS]
-                    for m in range(OUT_BLOCKS):
-                        nc.tensor.matmul(
-                            acc[m][:], w_node[:, 0, m * P:(m + 1) * P], table_T[:].indirect(source),
-                            start=False, stop=False,
-                        )
-                        nc.tensor.matmul(
-                            acc[m][:], w_node[:, 1, m * P:(m + 1) * P], table_T[:].indirect(target),
-                            start=False, stop=True,
-                        )
-                        e1 = result_ring.tile([P, PIECE], F32, name="e1")
-                        nc.scalar.activation(e1[:], acc[m][:], FUNC.Silu, bias=b_lin_sb[:, m:m + 1])
-                        product = result_ring.tile([P, PIECE], F32, name="product")
-                        nc.vector.tensor_tensor(product[:], e1[:], q_sb[:, m, :], MULT)
-                        nc.sync.dma_start(out[m * P:(m + 1) * P, c * PIECE:(c + 1) * PIECE], product[:])
+                    nc.tensor.matmul(
+                        acc[m][:], w_node[:, 1, m * P:(m + 1) * P], table_T[:].indirect(target),
+                        start=False, stop=True,
+                    )
+                    e1 = result_ring.tile([P, PIECE], F32, name="e1")
+                    nc.scalar.activation(e1[:], acc[m][:], FUNC.Silu, bias=b_lin_sb[:, m:m + 1])
+                    product = result_ring.tile([P, PIECE], F32, name="product")
+                    nc.vector.tensor_tensor(product[:], e1[:], q_sb[:, m, :], MULT)
+                    nc.sync.dma_start(out[m * P:(m + 1) * P, c * PIECE:(c + 1) * PIECE], product[:])

@@ -132,8 +132,9 @@ def tile_edgefeatureinit_b_kernel(tc, table, w_lin, b_lin, d, freq, w_rbf0, b_rb
                 acc = [acc_psum.tile([P, PIECE], F32, name="acc%d" % m) for m in range(OUT_BLOCKS)]
                 q_sb = held.tile([P, OUT_BLOCKS, PIECE], F32, name="q_sb%d" % c)
 
-            if c == 0 and b < N_STAGES:
-                flip_four(stages[b], table_T[:, b * GROUP:(b + 1) * GROUP], side_psum, "side")
+            if c == 0 and N_STAGES <= b < 2 * N_STAGES:
+                stage = b - N_STAGES
+                flip_four(stages[stage], table_T[:, stage * GROUP:(stage + 1) * GROUP], side_psum, "side")
             if b < OUT_BLOCKS:
                 q_ps = side_psum.tile([P, PIECE], F32, name="q_ps", tag="side")
                 nc.tensor.matmul(

@@ -160,8 +160,12 @@ def tile_edgefeatureinit_b_kernel(tc, table, w_lin, b_lin, d, freq, w_rbf0, b_rb
                         acc[m][:], w_node[:, 1, m * P:(m + 1) * P], table_T[:].indirect(target),
                         start=False, stop=True,
                     )
+                    last_block = c == N_PIECES - 1 and m == OUT_BLOCKS - 1
+                    width = PIECE // 2 if last_block else PIECE
                     e1 = result_ring.tile([P, PIECE], F32, name="e1")
-                    nc.scalar.activation(e1[:], acc[m][:], FUNC.Silu, bias=b_lin_sb[:, m:m + 1])
                     product = result_ring.tile([P, PIECE], F32, name="product")
-                    nc.vector.tensor_tensor(product[:], e1[:], q_sb[:, m, :], MULT)
+                    for first in range(0, PIECE, width):
+                        cols = slice(first, first + width)
+                        nc.scalar.activation(e1[:, cols], acc[m][:, cols], FUNC.Silu, bias=b_lin_sb[:, m:m + 1])
+                        nc.vector.tensor_tensor(product[:, cols], e1[:, cols], q_sb[:, m, cols], MULT)
                     nc.sync.dma_start(out[m * P:(m + 1) * P, c * PIECE:(c + 1) * PIECE], product[:])

import concourse.mybir as mybir
from concourse.masks import make_identity

BF16 = mybir.dt.bfloat16
F32 = mybir.dt.float32
U16 = mybir.dt.uint16
FUNC = mybir.ActivationFunctionType
MULT = mybir.AluOpType.mult

P = 128
NODES = 4096
FEAT = 128
RADIAL = 128
HIDDEN = 4096
OUT_FEAT = 512
EDGES = 1024
NORM = (2.0 / 5.0) ** 0.5

PIECE = 512
N_PIECES = EDGES // PIECE
PIECE_COLS = PIECE // 16
OUT_BLOCKS = OUT_FEAT // P
FOUR = 4
GROUP = FOUR * P
N_STAGES = NODES // GROUP
N_CHUNKS = HIDDEN // GROUP
HID_BLOCKS = HIDDEN // P
AHEAD = 2

FLOPS = 2 * EDGES * (RADIAL * HIDDEN + (2 * FEAT + HIDDEN) * OUT_FEAT + RADIAL * OUT_FEAT)


def tile_edgefeatureinit_b_kernel(tc, table, w_lin, b_lin, d, freq, w_rbf0, b_rbf0, w_rbf1, offs, out):
    nc = tc.nc
    with (
        tc.tile_pool(name="held", bufs=1) as held,
        tc.tile_pool(name="hidden_ring", bufs=4) as hidden_ring,
        tc.tile_pool(name="result_ring", bufs=4) as result_ring,
        tc.psum_pool(name="acc_psum", bufs=1) as acc_psum,
        tc.psum_pool(name="pre_psum", bufs=2) as pre_psum,
        tc.psum_pool(name="side_psum", bufs=2) as side_psum,
    ):

        d_col = held.tile([P, N_PIECES, FOUR], F32, name="d_col")
        nc.sync.dma_start(d_col[:], d.rearrange("o (c p i) -> p c (o i)", c=N_PIECES, i=FOUR))
        freq_row = held.tile([P, RADIAL], F32, name="freq_row")
        nc.scalar.dma_start(freq_row[:], freq.rearrange("r o -> (r o)").partition_broadcast(P))

        scratch = held.tile([P, 2], F32, name="scratch")
        nc.vector.memset(scratch[:], 0.0)

        def load_table_of(func):
            nc.scalar.activation(scratch[:, 1:2], scratch[:, 0:1], func)

        load_table_of(FUNC.Silu)

        identity = held.tile([P, P], BF16, name="identity")
        make_identity(nc, identity[:])

        b_rbf0_sb = held.tile([P, N_CHUNKS, FOUR], F32, name="b_rbf0_sb")
        w_rbf1_sb = held.tile([P, OUT_FEAT], BF16, name="w_rbf1_sb")

        assert N_STAGES == N_CHUNKS
        w_first = []
        w_hidden = []
        stages = []
        for g in range(N_CHUNKS):
            first = held.tile([P, GROUP], BF16, name="w_first%d" % g)
            nc.sync.dma_start(first[:], w_rbf0[:, g * GROUP:(g + 1) * GROUP])
            w_first.append(first[:].rearrange("r (p a) -> r a p", a=FOUR))
            if g == 0:
                nc.sync.dma_start(b_rbf0_sb[:], b_rbf0.rearrange("(g p a) o -> p g (a o)", g=N_CHUNKS, a=FOUR))
                nc.sync.dma_start(w_rbf1_sb[:], w_rbf1)
            hidden_rows = held.tile([P, FOUR, OUT_FEAT], BF16, name="w_hidden%d" % g)
            rows = w_lin[2 * FEAT + g * GROUP:2 * FEAT + (g + 1) * GROUP, :]
            nc.sync.dma_start(hidden_rows[:], rows.rearrange("(p a) m -> p a m", a=FOUR))
            w_hidden.append(hidden_rows)
            stage = held.tile([P, FOUR, FEAT], BF16, name="stage%d" % g)
            nc.sync.dma_start(stage[:], table[g * GROUP:(g + 1) * GROUP, :].rearrange("(p i) k -> p i k", i=FOUR))
            stages.append(stage)

        offsets = held.tile([P, 2 * EDGES // 16], U16, name="offsets")
        nc.sync.dma_start(offsets[:], offs)
        w_node = held.tile([P, 2, OUT_FEAT], BF16, name="w_node")
        nc.sync.dma_start(w_node[:], w_lin[0:2 * FEAT, :].rearrange("(s k) m -> k s m", s=2))
        b_lin_sb = held.tile([P, OUT_BLOCKS], F32, name="b_lin_sb")
        with nc.allow_non_contiguous_dma(reason="512 bias values, one to a partition and block"):
            nc.sync.dma_start(b_lin_sb[:], b_lin.rearrange("(a p) o -> p (a o)", p=P))

        def flip_four(blocks, flipped, psum, tag):
            bank = psum.tile([P, FOUR, P], BF16, name="flip_ps", tag=tag)
            for i in range(FOUR):
                nc.tensor.transpose(bank[:, i, :], blocks[:, i, :], identity[:])
            nc.vector.tensor_copy(flipped.rearrange("k (p i) -> k p i", i=FOUR), bank[:].rearrange("k i p -> k p i"))

        inv_d = held.tile([P, N_PIECES, FOUR], F32, name="inv_d")
        nc.vector.reciprocal(inv_d[:], d_col[:])
        sine = held.tile([P, N_PIECES, FOUR, RADIAL], F32, name="sine")
        for c in range(N_PIECES):
            for i in range(FOUR):
                nc.scalar.activation(sine[:, c, i, :], freq_row[:], FUNC.Sin, scale=d_col[:, c, i:i + 1])
        rbf = [held.tile([P, PIECE], BF16, name="rbf%d" % c) for c in range(N_PIECES)]

        def radial_basis(c):
            by_edge = held.tile([P, FOUR, RADIAL], BF16, name="by_edge%d" % c)
            for i in range(FOUR):
                nc.vector.tensor_scalar(
                    out=by_edge[:, i, :], in0=sine[:, c, i, :], scalar1=inv_d[:, c, i:i + 1], scalar2=NORM,
                    op0=MULT, op1=MULT,
                )
            flip_four(by_edge, rbf[c][:], acc_psum, "acc%d" % c)

        def hidden_block(c, b):
            g, a = divmod(b, FOUR)
            pre = pre_psum.tile([P, PIECE], F32, name="pre")
            nc.tensor.matmul(pre[:], w_first[g][:, a, :], rbf[c][:], start=True, stop=True)
            rbf0 = hidden_ring.tile([P, PIECE], BF16, name="rbf0")
            nc.scalar.activation(rbf0[:], pre[:], FUNC.Silu, bias=b_rbf0_sb[:, g, a:a + 1])
            return rbf0

        table_T = held.tile([P, NODES], BF16, name="table_T")
        steps = [(c, b) for c in range(N_PIECES) for b in range(HID_BLOCKS)]
        radial_basis(0)
        waiting = [hidden_block(c, b) for (c, b) in steps[:AHEAD]]
        radial_basis(1)

        for t, (c, b) in enumerate(steps):
            if t + AHEAD < len(steps):
                waiting.append(hidden_block(*steps[t + AHEAD]))

            if b == 0:
                acc = [acc_psum.tile([P, PIECE], F32, name="acc%d" % m) for m in range(OUT_BLOCKS)]
                q_sb = held.tile([P, OUT_BLOCKS, PIECE], F32, name="q_sb%d" % c)

            if c == 0 and N_STAGES <= b < 2 * N_STAGES:
                stage = b - N_STAGES
                flip_four(stages[stage], table_T[:, stage * GROUP:(stage + 1) * GROUP], side_psum, "side")
            if b < OUT_BLOCKS:
                q_ps = side_psum.tile([P, PIECE], F32, name="q_ps", tag="side")
                nc.tensor.matmul(
                    q_ps[:], w_rbf1_sb[:, b * P:(b + 1) * P], rbf[c][:], start=True, stop=True
                )
                nc.vector.tensor_copy(q_sb[:, b, :], q_ps[:])

            for m in range(OUT_BLOCKS):
                nc.tensor.matmul(
                    acc[m][:], w_hidden[b // FOUR][:, b % FOUR, m * P:(m + 1) * P], waiting[t][:],
                    start=(b == 0), stop=False,
                )

            if b == HID_BLOCKS - 1:
                source = offsets[:, c * PIECE_COLS:(c + 1) * PIECE_COLS]
                target = offsets[:, (N_PIECES + c) * PIECE_COLS:(N_PIECES + c + 1) * PIECE_COLS]
                for m in range(OUT_BLOCKS):
                    nc.tensor.matmul(
                        acc[m][:], w_node[:, 0, m * P:(m + 1) * P], table_T[:].indirect(source),
                        start=False, stop=False,
                    )
                    nc.tensor.matmul(
                        acc[m][:], w_node[:, 1, m * P:(m + 1) * P], table_T[:].indirect(target),
                        start=False, stop=True,
                    )
                    last_block = c == N_PIECES - 1 and m == OUT_BLOCKS - 1
                    width = PIECE // 2 if last_block else PIECE
                    e1 = result_ring.tile([P, PIECE], F32, name="e1")
                    product = result_ring.tile([P, PIECE], F32, name="product")
                    for first in range(0, PIECE, width):
                        cols = slice(first, first + width)
                        nc.scalar.activation(e1[:, cols], acc[m][:, cols], FUNC.Silu, bias=b_lin_sb[:, m:m + 1])
                        nc.vector.tensor_tensor(product[:, cols], e1[:, cols], q_sb[:, m, cols], MULT)
                    nc.sync.dma_start(out[m * P:(m + 1) * P, c * PIECE:(c + 1) * PIECE], product[:])
